import numpy as np
import ml_dtypes


def mxq(x, axis, fmt="e4m3"):
    dtype, down = {"e4m3": (ml_dtypes.float8_e4m3fn, 7), "e5m2": (ml_dtypes.float8_e5m2, 14)}[fmt]
    v = np.moveaxis(np.asarray(x, np.float32).astype(ml_dtypes.bfloat16).astype(np.float64), axis, -1)
    blocks = v.reshape(v.shape[:-1] + (-1, 32))
    amax = np.abs(blocks).max(-1, keepdims=True)
    byte = np.maximum(np.where(amax > 0, np.frexp(amax)[1] - 1 + 127, 0) - down, 1)
    scale = np.exp2(byte - 127.0)
    codes = (blocks / scale).astype(np.float32).astype(dtype).astype(np.float64)
    return np.moveaxis((codes * scale).reshape(v.shape), -1, axis)


WIDE = False


def mx_kscale(k):
    if not WIDE:
        return np.ones(k)
    levels = np.array([10, -10, 5, -5, 0])
    a = np.random.permutation(np.resize(levels, k // 512 * 4)).reshape(k // 512, 4)
    idx = np.arange(k)
    return np.exp2(a[idx // 512, idx % 128 // 32])


BF16 = ml_dtypes.bfloat16


def bf(x):
    return np.asarray(x, np.float32).astype(BF16)


def f64(x):
    return np.asarray(x).astype(np.float64)


B, F, C, DEPTH, LQ = 2048, 1024, 1024, 11, 7
NL = 2 ** (DEPTH - 1)
NQ = 2 ** LQ


def sigmoid(v):
    return 1.0 / (1.0 + np.exp(-v))


def setup_inputs():
    s = mx_kscale(F)
    return {"x": bf(np.random.standard_normal((B, F)) * s),
            "W_gate": bf(np.random.standard_normal((F, NL - 1)) * 2.0 / np.sqrt(F) / s[:, None]),
            "b_gate": bf(np.random.standard_normal(NL - 1) * 0.5),
            "leaf_logits": bf(np.random.standard_normal((NL, C)) * 0.5 * 1.2 ** (DEPTH - 1))}


def reference(x, W_gate, b_gate, leaf_logits):
    nb = x.shape[0]
    xf, wf = f64(x), f64(W_gate)
    top = (xf @ wf[:, :NQ])[:, :NQ - 1]
    low = mxq(xf, 1, "e4m3") @ mxq(wf[:, NQ - 1:], 0, "e4m3")
    p = sigmoid(np.concatenate([top, low], axis=1) + f64(b_gate))
    probs = np.ones((nb, 1))
    for level in range(DEPTH - 1):
        n = 2 ** level
        start = n - 1
        pl = p[:, start:start + n]
        probs = np.stack([(1.0 - pl) * probs, pl * probs], axis=-1).reshape(nb, 2 * n)
    return mxq(probs, 1, "e4m3") @ mxq(f64(leaf_logits), 0, "e4m3")

@@ -1,0 +1,268 @@
+from contextlib import ExitStack
+
+import concourse.mybir as mybir
+from concourse.masks import make_identity
+
+F32 = mybir.dt.float32
+BF16 = mybir.dt.bfloat16
+U32 = mybir.dt.uint32
+U8 = mybir.dt.uint8
+FP8X4 = mybir.dt.float8_e4m3fn_x4
+ALU = mybir.AluOpType
+SIGMOID = mybir.ActivationFunctionType.Sigmoid
+
+P = 128
+PACK = 4
+BANK = 512
+BATCH, FEATURES, LEAVES, CLASSES = 2048, 1024, 1024, 1024
+PASSES = 2
+CHUNK = BANK
+TILES = CHUNK // P
+CHUNKS = BATCH // CHUNK
+TOP_LEVELS = 7
+LOW_LEVELS = 3
+PLANES = 2**LOW_LEVELS - 1
+
+FLOPS = 2 * BATCH * FEATURES * 1024 + 2 * BATCH * LEAVES * CLASSES
+
+
+def tile_treemodel_kernel(tc, x, W_gate, b_gate, leaf_logits, out):
+    nc = tc.nc
+    with ExitStack() as ctx:
+        keep = ctx.enter_context(tc.tile_pool(name="keep", bufs=1))
+        x_in = ctx.enter_context(tc.tile_pool(name="x_in", bufs=CHUNKS))
+        stage = ctx.enter_context(tc.tile_pool(name="stage", bufs=2))
+        x_mx = ctx.enter_context(tc.tile_pool(name="x_mx", bufs=2))
+        top = ctx.enter_context(tc.tile_pool(name="top", bufs=1))
+        gates = ctx.enter_context(tc.tile_pool(name="gates", bufs=2))
+        low = ctx.enter_context(tc.tile_pool(name="low", bufs=1))
+        probs_mx = ctx.enter_context(tc.tile_pool(name="probs_mx", bufs=2))
+        result = ctx.enter_context(tc.tile_pool(name="result", bufs=4))
+        psum_xt = ctx.enter_context(tc.psum_pool(name="psum_xt", bufs=2))
+        psum_top = ctx.enter_context(tc.psum_pool(name="psum_top", bufs=1))
+        psum_gate = ctx.enter_context(tc.psum_pool(name="psum_gate", bufs=2))
+        psum_out = ctx.enter_context(tc.psum_pool(name="psum_out", bufs=2))
+
+        x_rows = x.rearrange("(c p i) k -> c p (i k)", p=P, i=TILES)
+        out_rows = out.rearrange("(c p i) n -> c p i n", p=P, i=TILES)
+
+        ident = keep.tile([P, P], F32)
+        make_identity(nc, ident[:])
+        ones = keep.tile([P, P], BF16)
+        nc.vector.memset(ones[:], 1.0)
+        bias_top = keep.tile([P, P], BF16)
+        nc.vector.memset(bias_top[:], 0.0)
+        nc.scalar.dma_start(out=bias_top[0:1, :], in_=b_gate[0:P].rearrange("(o n) -> o n", o=1))
+        bias_low = keep.tile([P, LOW_LEVELS, 16], BF16)
+        for a in range(LOW_LEVELS):
+            planes = 2**a
+            first_node = P * planes - 1
+            nc.scalar.dma_start(
+                out=bias_low[:, a, 0:planes],
+                in_=b_gate[first_node : first_node + P * planes].rearrange("(p m) -> p m", m=planes),
+            )
+
+        def load_x(c):
+            x_sb = x_in.tile([P, TILES, FEATURES], BF16)
+            nc.sync.dma_start(out=x_sb[:].rearrange("p i k -> p (i k)"), in_=x_rows[c])
+            return x_sb
+
+        x_chunks = [load_x(0)]
+        w_rows = keep.tile([P, PASSES * PACK, 1023], BF16)
+        nc.sync.dma_start(
+            out=w_rows[:].rearrange("p (j e) n -> p j (e n)", e=2),
+            in_=W_gate.rearrange("(j p e) n -> p j (e n)", p=P, e=2),
+        )
+        x_chunks.append(load_x(1))
+        leaf_rows = keep.tile([P, 2 * PACK, CLASSES], BF16)
+        nc.sync.dma_start(
+            out=leaf_rows[:].rearrange("p r n -> p (r n)"), in_=leaf_logits.rearrange("(p r) n -> p (r n)", p=P)
+        )
+        x_chunks.append(load_x(2))
+        x_chunks.append(load_x(3))
+
+        def prepare_x(c):
+            x_sb = x_chunks[c]
+            x_grouped = x_mx.tile([P, PASSES, CHUNK, PACK], BF16, align_bytes=64)
+            x_pairs = x_grouped[:].bitcast(F32)
+            for i in range(TILES):
+                xt = psum_xt.tile([P, PASSES * 2, P], F32)
+                for j in range(PASSES * 2):
+                    nc.tensor.transpose(xt[:, j, :], x_sb[:, i, :].bitcast(F32)[:, j * P : (j + 1) * P], ident[:])
+                nc.vector.tensor_copy(
+                    out=x_pairs[:, :, i * P : (i + 1) * P, :], in_=xt[:].rearrange("p (g u) b -> p g b u", u=2)
+                )
+            x_codes = x_mx.tile([P, PASSES, CHUNK], U32, align_bytes=64)
+            x_scales = x_mx.tile([P, PASSES, CHUNK], U8, align_bytes=64)
+            for g in range(PASSES):
+                nc.vector.quantize_mx(
+                    out=x_codes[:, g, :].bitcast(FP8X4),
+                    scales=x_scales[:, g, :],
+                    in_=x_grouped[:, g].rearrange("p b t -> p (b t)"),
+                )
+            return x_grouped, x_codes, x_scales
+
+        w_codes = keep.tile([P, PASSES, PLANES * P], U32, align_bytes=64)
+        w_scales = keep.tile([P, PASSES, PLANES * P], U8, align_bytes=64)
+
+        def prepare_w():
+            grouped = []
+            for g in range(PASSES):
+                w_grouped = stage.tile([P, PLANES, P, PACK], BF16, align_bytes=64)
+                for a in range(LOW_LEVELS):
+                    planes = 2**a
+                    first_node = P * planes - 1
+                    nc.vector.tensor_copy(
+                        out=w_grouped[:, planes - 1 : 2 * planes - 1],
+                        in_=w_rows[:, g * PACK : (g + 1) * PACK, first_node : first_node + P * planes].rearrange(
+                            "p t (j m) -> p m j t", m=planes
+                        ),
+                    )
+                grouped.append(w_grouped)
+            for g in range(PASSES):
+                for a in range(LOW_LEVELS):
+                    planes = 2**a
+                    cols = slice((planes - 1) * P, (2 * planes - 1) * P)
+                    nc.vector.quantize_mx(
+                        out=w_codes[:, g, cols].bitcast(FP8X4),
+                        scales=w_scales[:, g, cols],
+                        in_=grouped[g][:, planes - 1 : 2 * planes - 1].rearrange("p m j t -> p (m j t)"),
+                    )
+
+        leaf_codes = keep.tile([P, PASSES, CLASSES], U32, align_bytes=64)
+        leaf_scales = keep.tile([P, PASSES, CLASSES], U8, align_bytes=64)
+
+        def prepare_leaves():
+            for s in range(PASSES):
+                for h in range(CLASSES // BANK):
+                    cols = slice(h * BANK, (h + 1) * BANK)
+                    leaf_grouped = stage.tile([P, BANK, PACK], BF16, align_bytes=64)
+                    nc.scalar.copy(
+                        out=leaf_grouped[:].rearrange("p (n i) t -> p n t i", i=4),
+                        in_=leaf_rows[:].rearrange("p (t s) n -> p s t n", s=PASSES)[:, s, :, cols].rearrange(
+                            "p t (n i) -> p n t i", i=4
+                        ),
+                    )
+                    nc.vector.quantize_mx(
+                        out=leaf_codes[:, s, cols].bitcast(FP8X4),
+                        scales=leaf_scales[:, s, cols],
+                        in_=leaf_grouped[:].rearrange("p n t -> p (n t)"),
+                    )
+
+        def top_logits(x_grouped):
+            z_top = psum_top.tile([P, TILES, P], F32)
+            for i in range(TILES):
+                for r in range(PASSES * PACK):
+                    nc.tensor.matmul(
+                        out=z_top[:, i, :],
+                        lhsT=x_grouped[:, r // PACK, i * P : (i + 1) * P, r % PACK],
+                        rhs=w_rows[:, r, 0:P],
+                        start=(r == 0),
+                        stop=False,
+                    )
+                nc.tensor.matmul(out=z_top[:, i, :], lhsT=ones[:], rhs=bias_top[:], start=False, stop=True)
+            return z_top
+
+        def top_sweep(z_top):
+            turn = top.tile([P, 2, TILES, P], F32)
+            nc.scalar.activation(out=turn[:, 1], in_=z_top[:], func=SIGMOID)
+            nc.scalar.activation(out=turn[:, 0], in_=z_top[:], func=SIGMOID, scale=-1.0)
+            reach = turn[:, :, :, 0].rearrange("p s i -> p i s")
+            for level in range(1, TOP_LEVELS):
+                n = 2**level
+                children = top.tile([P, TILES, n, 2], F32, name="reach%d" % (level + 1))
+                nc.vector.tensor_tensor(
+                    out=children[:],
+                    in0=turn[:, :, :, n - 1 : 2 * n - 1].rearrange("p s i j -> p i j s"),
+                    in1=reach.unsqueeze(3).to_broadcast([P, TILES, n, 2]),
+                    op=ALU.mult,
+                )
+                reach = children[:].rearrange("p i j s -> p i (j s)")
+            reach7 = psum_top.tile([P, CHUNK], F32)
+            for i in range(TILES):
+                nc.tensor.transpose(reach7[:, i * P : (i + 1) * P], reach[:, i, :], ident[:])
+            return reach7
+
+        def low_gates(x_codes, x_scales):
+            gate = gates.tile([P, PLANES, CHUNK], F32)
+            for a in range(LOW_LEVELS):
+                for m in range(2**a):
+                    plane = 2**a - 1 + m
+                    z = psum_gate.tile([P, CHUNK], F32)
+                    for g in range(PASSES):
+                        nc.tensor.matmul_mx(
+                            out=z[:],
+                            lhsT=w_codes[:, g, plane * P : (plane + 1) * P].bitcast(FP8X4),
+                            lhsT_scale=w_scales[:, g, plane * P : (plane + 1) * P],
+                            rhs=x_codes[:, g, :].bitcast(FP8X4),
+                            rhs_scale=x_scales[:, g, :],
+                            start=(g == 0),
+                            stop=(g == PASSES - 1),
+                        )
+                    nc.scalar.activation(out=gate[:, plane, :], in_=z[:], func=SIGMOID, bias=bias_low[:, a, m : m + 1])
+            return gate
+
+        def split_flipping_sign(left, right, p_right, parent):
+            nc.vector.scalar_tensor_tensor(
+                out=left, in0=p_right, scalar=1.0, in1=parent, op0=ALU.subtract, op1=ALU.mult
+            )
+            nc.vector.scalar_tensor_tensor(out=right, in0=p_right, scalar=-1.0, in1=parent, op0=ALU.mult, op1=ALU.mult)
+
+        def low_sweep(gate, reach7):
+            reach8 = low.tile([P, 2, CHUNK], F32)
+            nc.vector.tensor_tensor(out=reach8[:, 1, :], in0=gate[:, 0, :], in1=reach7[:], op=ALU.mult)
+            nc.vector.tensor_tensor(out=reach8[:, 0, :], in0=reach7[:], in1=reach8[:, 1, :], op=ALU.subtract)
+            minus_reach9 = low.tile([P, 2, 2, CHUNK], F32)
+            split_flipping_sign(minus_reach9[:, :, 0, :], minus_reach9[:, :, 1, :], gate[:, 1:3, :], reach8[:])
+            probs_grouped = low.tile([P, PASSES, CHUNK, PACK], BF16, align_bytes=64)
+            split_flipping_sign(
+                probs_grouped[:, 0],
+                probs_grouped[:, 1],
+                gate[:, 3:7, :].rearrange("p t b -> p b t"),
+                minus_reach9[:].rearrange("p s2 s1 b -> p b (s2 s1)"),
+            )
+            probs_codes = probs_mx.tile([P, PASSES, CHUNK], U32, align_bytes=64)
+            probs_scales = probs_mx.tile([P, PASSES, CHUNK], U8, align_bytes=64)
+            for s in range(PASSES):
+                nc.vector.quantize_mx(
+                    out=probs_codes[:, s, :].bitcast(FP8X4),
+                    scales=probs_scales[:, s, :],
+                    in_=probs_grouped[:, s].rearrange("p b t -> p (b t)"),
+                )
+            return probs_codes, probs_scales
+
+        def leaf_product(c, probs_codes, probs_scales):
+            for i in range(TILES):
+                out_sb = result.tile([P, CLASSES], F32)
+                for h in range(CLASSES // BANK):
+                    cols = slice(h * BANK, (h + 1) * BANK)
+                    acc = psum_out.tile([P, BANK], F32)
+                    for s in range(PASSES):
+                        nc.tensor.matmul_mx(
+                            out=acc[:],
+                            lhsT=probs_codes[:, s, i * P : (i + 1) * P].bitcast(FP8X4),
+                            lhsT_scale=probs_scales[:, s, i * P : (i + 1) * P],
+                            rhs=leaf_codes[:, s, cols].bitcast(FP8X4),
+                            rhs_scale=leaf_scales[:, s, cols],
+                            start=(s == 0),
+                            stop=(s == PASSES - 1),
+                        )
+                    nc.scalar.copy(out=out_sb[:, cols], in_=acc[:])
+                nc.sync.dma_start(out=out_rows[c][:, i, :], in_=out_sb[:])
+
+        x_grouped, x_codes, x_scales = prepare_x(0)
+        prepare_w()
+        z_top = top_logits(x_grouped)
+        gate = low_gates(x_codes, x_scales)
+        reach7 = top_sweep(z_top)
+        prepare_leaves()
+        for c in range(CHUNKS):
+            if c + 1 < CHUNKS:
+                x_grouped, x_codes, x_scales = prepare_x(c + 1)
+            probs_codes, probs_scales = low_sweep(gate, reach7)
+            if c + 1 < CHUNKS:
+                z_top = top_logits(x_grouped)
+                gate = low_gates(x_codes, x_scales)
+            leaf_product(c, probs_codes, probs_scales)
+            if c + 1 < CHUNKS:
+                reach7 = top_sweep(z_top)

@@ -17,6 +17,7 @@ BANK = 512
 BATCH, FEATURES, LEAVES, CLASSES = 2048, 1024, 1024, 1024
 PASSES = 2
 CHUNK = BANK
+HALF = CHUNK // 2
 TILES = CHUNK // P
 CHUNKS = BATCH // CHUNK
 TOP_LEVELS = 7
@@ -38,10 +39,8 @@ def tile_treemodel_kernel(tc, x, W_gate, b_gate, leaf_logits, out):
         low = ctx.enter_context(tc.tile_pool(name="low", bufs=1))
         probs_mx = ctx.enter_context(tc.tile_pool(name="probs_mx", bufs=2))
         result = ctx.enter_context(tc.tile_pool(name="result", bufs=4))
-        psum_xt = ctx.enter_context(tc.psum_pool(name="psum_xt", bufs=2))
         psum_top = ctx.enter_context(tc.psum_pool(name="psum_top", bufs=1))
-        psum_gate = ctx.enter_context(tc.psum_pool(name="psum_gate", bufs=2))
-        psum_out = ctx.enter_context(tc.psum_pool(name="psum_out", bufs=2))
+        psum_ring = ctx.enter_context(tc.psum_pool(name="psum_ring", bufs=6))
 
         x_rows = x.rearrange("(c p i) k -> c p (i k)", p=P, i=TILES)
         out_rows = out.rearrange("(c p i) n -> c p i n", p=P, i=TILES)
@@ -68,11 +67,13 @@ def tile_treemodel_kernel(tc, x, W_gate, b_gate, leaf_logits, out):
             return x_sb
 
         x_chunks = [load_x(0)]
-        w_rows = keep.tile([P, PASSES * PACK, 1023], BF16)
-        nc.sync.dma_start(
-            out=w_rows[:].rearrange("p (j e) n -> p j (e n)", e=2),
-            in_=W_gate.rearrange("(j p e) n -> p j (e n)", p=P, e=2),
-        )
+        w_rows = []
+        for g in range(PASSES):
+            w_rows.append(keep.tile([P, PACK, 1023], BF16, name="w_rows%d" % g))
+            nc.sync.dma_start(
+                out=w_rows[g][:].rearrange("p (u e) n -> p u (e n)", e=2),
+                in_=W_gate.rearrange("(g u p e) n -> g p u (e n)", g=PASSES, p=P, e=2)[g],
+            )
         x_chunks.append(load_x(1))
         leaf_rows = keep.tile([P, 2 * PACK, CLASSES], BF16)
         nc.sync.dma_start(
@@ -81,26 +82,31 @@ def tile_treemodel_kernel(tc, x, W_gate, b_gate, leaf_logits, out):
         x_chunks.append(load_x(2))
         x_chunks.append(load_x(3))
 
-        def prepare_x(c):
-            x_sb = x_chunks[c]
-            x_grouped = x_mx.tile([P, PASSES, CHUNK, PACK], BF16, align_bytes=64)
-            x_pairs = x_grouped[:].bitcast(F32)
+        x_grouped, x_codes, x_scales, z_top, turn, reach, reach7, gate = {}, {}, {}, {}, {}, {}, {}, {}
+        minus_reach9, probs_grouped, probs_codes, probs_scales = {}, {}, {}, {}
+
+        def transpose_x(c):
+            x_grouped[c] = x_mx.tile([P, PASSES, CHUNK, PACK], BF16, align_bytes=64, name="x_grouped")
+            x_pairs = x_grouped[c][:].bitcast(F32)
             for i in range(TILES):
-                xt = psum_xt.tile([P, PASSES * 2, P], F32)
+                xt = psum_ring.tile([P, PASSES * 2, P], F32, tag="ring")
                 for j in range(PASSES * 2):
-                    nc.tensor.transpose(xt[:, j, :], x_sb[:, i, :].bitcast(F32)[:, j * P : (j + 1) * P], ident[:])
-                nc.vector.tensor_copy(
+                    nc.tensor.transpose(
+                        xt[:, j, :], x_chunks[c][:, i, :].bitcast(F32)[:, j * P : (j + 1) * P], ident[:]
+                    )
+                nc.scalar.copy(
                     out=x_pairs[:, :, i * P : (i + 1) * P, :], in_=xt[:].rearrange("p (g u) b -> p g b u", u=2)
                 )
-            x_codes = x_mx.tile([P, PASSES, CHUNK], U32, align_bytes=64)
-            x_scales = x_mx.tile([P, PASSES, CHUNK], U8, align_bytes=64)
+
+        def quantise_x(c):
+            x_codes[c] = x_mx.tile([P, PASSES, CHUNK], U32, align_bytes=64, name="x_codes")
+            x_scales[c] = x_mx.tile([P, PASSES, CHUNK], U8, align_bytes=64, name="x_scales")
             for g in range(PASSES):
                 nc.vector.quantize_mx(
-                    out=x_codes[:, g, :].bitcast(FP8X4),
-                    scales=x_scales[:, g, :],
-                    in_=x_grouped[:, g].rearrange("p b t -> p (b t)"),
+                    out=x_codes[c][:, g, :].bitcast(FP8X4),
+                    scales=x_scales[c][:, g, :],
+                    in_=x_grouped[c][:, g].rearrange("p b t -> p (b t)"),
                 )
-            return x_grouped, x_codes, x_scales
 
         w_codes = keep.tile([P, PASSES, PLANES * P], U32, align_bytes=64)
         w_scales = keep.tile([P, PASSES, PLANES * P], U8, align_bytes=64)
@@ -112,15 +118,16 @@ def tile_treemodel_kernel(tc, x, W_gate, b_gate, leaf_logits, out):
                 for a in range(LOW_LEVELS):
                     planes = 2**a
                     first_node = P * planes - 1
-                    nc.vector.tensor_copy(
+                    copy = nc.vector.tensor_copy if a == LOW_LEVELS - 1 else nc.scalar.copy
+                    copy(
                         out=w_grouped[:, planes - 1 : 2 * planes - 1],
-                        in_=w_rows[:, g * PACK : (g + 1) * PACK, first_node : first_node + P * planes].rearrange(
+                        in_=w_rows[g][:, :, first_node : first_node + P * planes].rearrange(
                             "p t (j m) -> p m j t", m=planes
                         ),
                     )
                 grouped.append(w_grouped)
-            for g in range(PASSES):
-                for a in range(LOW_LEVELS):
+            for a in range(LOW_LEVELS):
+                for g in range(PASSES):
                     planes = 2**a
                     cols = slice((planes - 1) * P, (2 * planes - 1) * P)
                     nc.vector.quantize_mx(
@@ -132,116 +139,141 @@ def tile_treemodel_kernel(tc, x, W_gate, b_gate, leaf_logits, out):
         leaf_codes = keep.tile([P, PASSES, CLASSES], U32, align_bytes=64)
         leaf_scales = keep.tile([P, PASSES, CLASSES], U8, align_bytes=64)
 
-        def prepare_leaves():
-            for s in range(PASSES):
-                for h in range(CLASSES // BANK):
-                    cols = slice(h * BANK, (h + 1) * BANK)
-                    leaf_grouped = stage.tile([P, BANK, PACK], BF16, align_bytes=64)
-                    nc.scalar.copy(
-                        out=leaf_grouped[:].rearrange("p (n i) t -> p n t i", i=4),
-                        in_=leaf_rows[:].rearrange("p (t s) n -> p s t n", s=PASSES)[:, s, :, cols].rearrange(
-                            "p t (n i) -> p n t i", i=4
-                        ),
-                    )
-                    nc.vector.quantize_mx(
-                        out=leaf_codes[:, s, cols].bitcast(FP8X4),
-                        scales=leaf_scales[:, s, cols],
-                        in_=leaf_grouped[:].rearrange("p n t -> p (n t)"),
-                    )
+        leaf_grouped = {}
 
-        def top_logits(x_grouped):
-            z_top = psum_top.tile([P, TILES, P], F32)
-            for i in range(TILES):
-                for r in range(PASSES * PACK):
-                    nc.tensor.matmul(
-                        out=z_top[:, i, :],
-                        lhsT=x_grouped[:, r // PACK, i * P : (i + 1) * P, r % PACK],
-                        rhs=w_rows[:, r, 0:P],
-                        start=(r == 0),
-                        stop=False,
-                    )
-                nc.tensor.matmul(out=z_top[:, i, :], lhsT=ones[:], rhs=bias_top[:], start=False, stop=True)
-            return z_top
-
-        def top_sweep(z_top):
-            turn = top.tile([P, 2, TILES, P], F32)
-            nc.scalar.activation(out=turn[:, 1], in_=z_top[:], func=SIGMOID)
-            nc.scalar.activation(out=turn[:, 0], in_=z_top[:], func=SIGMOID, scale=-1.0)
-            reach = turn[:, :, :, 0].rearrange("p s i -> p i s")
-            for level in range(1, TOP_LEVELS):
-                n = 2**level
-                children = top.tile([P, TILES, n, 2], F32, name="reach%d" % (level + 1))
-                nc.vector.tensor_tensor(
-                    out=children[:],
-                    in0=turn[:, :, :, n - 1 : 2 * n - 1].rearrange("p s i j -> p i j s"),
-                    in1=reach.unsqueeze(3).to_broadcast([P, TILES, n, 2]),
-                    op=ALU.mult,
+        def regroup_leaves(s):
+            leaf_grouped[s] = stage.tile([P, CLASSES, PACK], BF16, align_bytes=64, name="leaf_grouped")
+            for h in range(CLASSES // BANK):
+                cols = slice(h * BANK, (h + 1) * BANK)
+                nc.scalar.copy(
+                    out=leaf_grouped[s][:, cols, :].rearrange("p (n i) t -> p n t i", i=4),
+                    in_=leaf_rows[:]
+                    .rearrange("p (t s) n -> p s t n", s=PASSES)[:, s, :, cols]
+                    .rearrange("p t (n i) -> p n t i", i=4),
                 )
-                reach = children[:].rearrange("p i j s -> p i (j s)")
-            reach7 = psum_top.tile([P, CHUNK], F32)
-            for i in range(TILES):
-                nc.tensor.transpose(reach7[:, i * P : (i + 1) * P], reach[:, i, :], ident[:])
-            return reach7
 
-        def low_gates(x_codes, x_scales):
-            gate = gates.tile([P, PLANES, CHUNK], F32)
+        def quantise_leaves(s):
+            nc.vector.quantize_mx(
+                out=leaf_codes[:, s, :].bitcast(FP8X4),
+                scales=leaf_scales[:, s, :],
+                in_=leaf_grouped[s][:].rearrange("p n t -> p (n t)"),
+            )
+
+        def top_logits(c):
+            z_top[c] = psum_top.tile([P, TILES, P], F32, name="z_top")
+            for i in range(TILES):
+                for g in range(PASSES):
+                    for t in range(PACK):
+                        nc.tensor.matmul(
+                            out=z_top[c][:, i, :],
+                            lhsT=x_grouped[c][:, g, i * P : (i + 1) * P, t],
+                            rhs=w_rows[g][:, t, 0:P],
+                            start=(g == 0 and t == 0),
+                            stop=False,
+                        )
+                nc.tensor.matmul(out=z_top[c][:, i, :], lhsT=ones[:], rhs=bias_top[:], start=False, stop=True)
+
+        def top_turns(c):
+            turn[c] = top.tile([P, 2, TILES, P], F32, name="turn")
+            nc.scalar.activation(out=turn[c][:, 1], in_=z_top[c][:], func=SIGMOID)
+            nc.scalar.activation(out=turn[c][:, 0], in_=z_top[c][:], func=SIGMOID, scale=-1.0)
+
+        def top_level(c, level):
+            n = 2**level
+            if level == 1:
+                reach[c] = turn[c][:, :, :, 0].rearrange("p s i -> p i s")
+            children = top.tile([P, TILES, n, 2], F32, name="children%d" % level)
+            nc.vector.tensor_tensor(
+                out=children[:],
+                in0=turn[c][:, :, :, n - 1 : 2 * n - 1].rearrange("p s i j -> p i j s"),
+                in1=reach[c].unsqueeze(3).to_broadcast([P, TILES, n, 2]),
+                op=ALU.mult,
+            )
+            reach[c] = children[:].rearrange("p i j s -> p i (j s)")
+
+        def top_transpose(c):
+            reach7[c] = psum_top.tile([P, CHUNK], F32, name="reach7")
+            for i in range(TILES):
+                nc.tensor.transpose(reach7[c][:, i * P : (i + 1) * P], reach[c][:, i, :], ident[:])
+
+        def low_gates(c):
+            gate[c] = gates.tile([P, PLANES, CHUNK], F32, name="gate")
             for a in range(LOW_LEVELS):
                 for m in range(2**a):
                     plane = 2**a - 1 + m
-                    z = psum_gate.tile([P, CHUNK], F32)
+                    z = psum_ring.tile([P, CHUNK], F32, tag="ring")
                     for g in range(PASSES):
                         nc.tensor.matmul_mx(
                             out=z[:],
                             lhsT=w_codes[:, g, plane * P : (plane + 1) * P].bitcast(FP8X4),
                             lhsT_scale=w_scales[:, g, plane * P : (plane + 1) * P],
-                            rhs=x_codes[:, g, :].bitcast(FP8X4),
-                            rhs_scale=x_scales[:, g, :],
+                            rhs=x_codes[c][:, g, :].bitcast(FP8X4),
+                            rhs_scale=x_scales[c][:, g, :],
                             start=(g == 0),
                             stop=(g == PASSES - 1),
                         )
-                    nc.scalar.activation(out=gate[:, plane, :], in_=z[:], func=SIGMOID, bias=bias_low[:, a, m : m + 1])
-            return gate
+                    nc.scalar.activation(
+                        out=gate[c][:, plane, :], in_=z[:], func=SIGMOID, bias=bias_low[:, a, m : m + 1]
+                    )
 
-        def split_flipping_sign(left, right, p_right, parent):
-            nc.vector.scalar_tensor_tensor(
-                out=left, in0=p_right, scalar=1.0, in1=parent, op0=ALU.subtract, op1=ALU.mult
-            )
-            nc.vector.scalar_tensor_tensor(out=right, in0=p_right, scalar=-1.0, in1=parent, op0=ALU.mult, op1=ALU.mult)
-
-        def low_sweep(gate, reach7):
-            reach8 = low.tile([P, 2, CHUNK], F32)
-            nc.vector.tensor_tensor(out=reach8[:, 1, :], in0=gate[:, 0, :], in1=reach7[:], op=ALU.mult)
-            nc.vector.tensor_tensor(out=reach8[:, 0, :], in0=reach7[:], in1=reach8[:, 1, :], op=ALU.subtract)
-            minus_reach9 = low.tile([P, 2, 2, CHUNK], F32)
-            split_flipping_sign(minus_reach9[:, :, 0, :], minus_reach9[:, :, 1, :], gate[:, 1:3, :], reach8[:])
-            probs_grouped = low.tile([P, PASSES, CHUNK, PACK], BF16, align_bytes=64)
-            split_flipping_sign(
-                probs_grouped[:, 0],
-                probs_grouped[:, 1],
-                gate[:, 3:7, :].rearrange("p t b -> p b t"),
-                minus_reach9[:].rearrange("p s2 s1 b -> p b (s2 s1)"),
-            )
-            probs_codes = probs_mx.tile([P, PASSES, CHUNK], U32, align_bytes=64)
-            probs_scales = probs_mx.tile([P, PASSES, CHUNK], U8, align_bytes=64)
-            for s in range(PASSES):
-                nc.vector.quantize_mx(
-                    out=probs_codes[:, s, :].bitcast(FP8X4),
-                    scales=probs_scales[:, s, :],
-                    in_=probs_grouped[:, s].rearrange("p b t -> p (b t)"),
+        def child_flipping_sign(s, child, p_right, parent):
+            if s == 0:
+                nc.vector.scalar_tensor_tensor(
+                    out=child, in0=p_right, scalar=1.0, in1=parent, op0=ALU.subtract, op1=ALU.mult
                 )
-            return probs_codes, probs_scales
+            else:
+                nc.vector.scalar_tensor_tensor(
+                    out=child, in0=p_right, scalar=-1.0, in1=parent, op0=ALU.mult, op1=ALU.mult
+                )
 
-        def leaf_product(c, probs_codes, probs_scales):
+        def sweep_levels_7_8(c):
+            minus_reach8 = low.tile([P, 2, CHUNK], F32)
+            for s3 in range(2):
+                child_flipping_sign(s3, minus_reach8[:, s3, :], gate[c][:, 0, :], reach7[c][:])
+            minus_reach9[c] = low.tile([P, 2, 2, CHUNK], F32, name="minus_reach9")
+            for s3 in range(2):
+                nc.vector.tensor_tensor(
+                    out=minus_reach9[c][:, s3, 1, :], in0=gate[c][:, 1 + s3, :], in1=minus_reach8[:, s3, :], op=ALU.mult
+                )
+            for s3 in range(2):
+                nc.vector.tensor_tensor(
+                    out=minus_reach9[c][:, s3, 0, :],
+                    in0=minus_reach8[:, s3, :],
+                    in1=minus_reach9[c][:, s3, 1, :],
+                    op=ALU.subtract,
+                )
+            probs_grouped[c] = low.tile([P, PASSES, CHUNK, PACK], BF16, align_bytes=64, name="probs_grouped")
+            probs_codes[c] = probs_mx.tile([P, PASSES, CHUNK], U32, align_bytes=64, name="probs_codes")
+            probs_scales[c] = probs_mx.tile([P, PASSES, CHUNK], U8, align_bytes=64, name="probs_scales")
+
+        def sweep_level_9(c, half, s):
+            rows = slice(half * HALF, (half + 1) * HALF)
+            child_flipping_sign(
+                s,
+                probs_grouped[c][:, s, rows, :],
+                gate[c][:, 3:7, rows].rearrange("p t b -> p b t"),
+                minus_reach9[c][:, :, :, rows].rearrange("p s3 s2 b -> p b (s3 s2)"),
+            )
+
+        def quantise_probs(c, half, s):
+            rows = slice(half * HALF, (half + 1) * HALF)
+            nc.vector.quantize_mx(
+                out=probs_codes[c][:, s, rows].bitcast(FP8X4),
+                scales=probs_scales[c][:, s, rows],
+                in_=probs_grouped[c][:, s, rows, :].rearrange("p b t -> p (b t)"),
+            )
+
+        def leaf_product(c):
             for i in range(TILES):
                 out_sb = result.tile([P, CLASSES], F32)
                 for h in range(CLASSES // BANK):
                     cols = slice(h * BANK, (h + 1) * BANK)
-                    acc = psum_out.tile([P, BANK], F32)
+                    acc = psum_ring.tile([P, BANK], F32, tag="ring")
                     for s in range(PASSES):
                         nc.tensor.matmul_mx(
                             out=acc[:],
-                            lhsT=probs_codes[:, s, i * P : (i + 1) * P].bitcast(FP8X4),
-                            lhsT_scale=probs_scales[:, s, i * P : (i + 1) * P],
+                            lhsT=probs_codes[c][:, s, i * P : (i + 1) * P].bitcast(FP8X4),
+                            lhsT_scale=probs_scales[c][:, s, i * P : (i + 1) * P],
                             rhs=leaf_codes[:, s, cols].bitcast(FP8X4),
                             rhs_scale=leaf_scales[:, s, cols],
                             start=(s == 0),
@@ -250,19 +282,38 @@ def tile_treemodel_kernel(tc, x, W_gate, b_gate, leaf_logits, out):
                     nc.scalar.copy(out=out_sb[:, cols], in_=acc[:])
                 nc.sync.dma_start(out=out_rows[c][:, i, :], in_=out_sb[:])
 
-        x_grouped, x_codes, x_scales = prepare_x(0)
-        prepare_w()
-        z_top = top_logits(x_grouped)
-        gate = low_gates(x_codes, x_scales)
-        reach7 = top_sweep(z_top)
-        prepare_leaves()
-        for c in range(CHUNKS):
-            if c + 1 < CHUNKS:
-                x_grouped, x_codes, x_scales = prepare_x(c + 1)
-            probs_codes, probs_scales = low_sweep(gate, reach7)
-            if c + 1 < CHUNKS:
-                z_top = top_logits(x_grouped)
-                gate = low_gates(x_codes, x_scales)
-            leaf_product(c, probs_codes, probs_scales)
-            if c + 1 < CHUNKS:
-                reach7 = top_sweep(z_top)
+        def in_range(c):
+            return 0 <= c < CHUNKS
+
+        with tc.manual_schedule():
+            for c in range(-2, CHUNKS + 1):
+                if in_range(c):
+                    sweep_levels_7_8(c)
+                if in_range(c + 1):
+                    quantise_x(c + 1)
+                if c == -1:
+                    prepare_w()
+                if c == 1:
+                    quantise_leaves(0)
+                    quantise_leaves(1)
+                if in_range(c + 1):
+                    top_logits(c + 1)
+                    top_turns(c + 1)
+                    low_gates(c + 1)
+                for half in range(2):
+                    if in_range(c):
+                        for s in range(PASSES):
+                            sweep_level_9(c, half, s)
+                        for s in range(PASSES):
+                            quantise_probs(c, half, s)
+                    if in_range(c + 1) and half == 0:
+                        for level in range(1, TOP_LEVELS):
+                            top_level(c + 1, level)
+                if in_range(c - 1):
+                    leaf_product(c - 1)
+                if in_range(c + 1):
+                    top_transpose(c + 1)
+                if in_range(c + 2):
+                    transpose_x(c + 2)
+                if c == -1 or c == 0:
+                    regroup_leaves(c + 1)

@@ -145,12 +145,16 @@ def tile_treemodel_kernel(tc, x, W_gate, b_gate, leaf_logits, out):
             leaf_grouped[s] = stage.tile([P, CLASSES, PACK], BF16, align_bytes=64, name="leaf_grouped")
             for h in range(CLASSES // BANK):
                 cols = slice(h * BANK, (h + 1) * BANK)
-                nc.scalar.copy(
-                    out=leaf_grouped[s][:, cols, :].rearrange("p (n i) t -> p n t i", i=4),
-                    in_=leaf_rows[:]
+                grouped = leaf_grouped[s][:, cols, :].rearrange("p (n i) t -> p n t i", i=4)
+                rows = (
+                    leaf_rows[:]
                     .rearrange("p (t s) n -> p s t n", s=PASSES)[:, s, :, cols]
-                    .rearrange("p t (n i) -> p n t i", i=4),
+                    .rearrange("p t (n i) -> p n t i", i=4)
                 )
+                if s == 0:
+                    nc.scalar.copy(out=grouped, in_=rows)
+                else:
+                    nc.scalar.mul(out=grouped, in_=rows, mul=-1.0)
 
         def quantise_leaves(s):
             nc.vector.quantize_mx(
@@ -248,12 +252,24 @@ def tile_treemodel_kernel(tc, x, W_gate, b_gate, leaf_logits, out):
 
         def sweep_level_9(c, half, s):
             rows = slice(half * HALF, (half + 1) * HALF)
-            child_flipping_sign(
-                s,
-                probs_grouped[c][:, s, rows, :],
-                gate[c][:, 3:7, rows].rearrange("p t b -> p b t"),
-                minus_reach9[c][:, :, :, rows].rearrange("p s3 s2 b -> p b (s3 s2)"),
-            )
+            right, parent = gate[c][:, 3:7, rows], minus_reach9[c][:, :, :, rows]
+            words = probs_grouped[c][:, s, rows, :]
+            if s == 0:
+                nc.vector.scalar_tensor_tensor(
+                    out=words,
+                    in0=right.rearrange("p t b -> p b t"),
+                    scalar=1.0,
+                    in1=parent.rearrange("p s3 s2 b -> p b (s3 s2)"),
+                    op0=ALU.subtract,
+                    op1=ALU.mult,
+                )
+            else:
+                nc.vector.tensor_tensor(
+                    out=words.rearrange("p (b i) t -> p b t i", i=4),
+                    in0=right.rearrange("p t (b i) -> p b t i", i=4),
+                    in1=parent.rearrange("p s3 s2 (b i) -> p b (s3 s2) i", i=4),
+                    op=ALU.mult,
+                )
 
         def quantise_probs(c, half, s):
             rows = slice(half * HALF, (half + 1) * HALF)

@@ -17,12 +17,12 @@ BANK = 512
 BATCH, FEATURES, LEAVES, CLASSES = 2048, 1024, 1024, 1024
 PASSES = 2
 CHUNK = BANK
-HALF = CHUNK // 2
 TILES = CHUNK // P
 CHUNKS = BATCH // CHUNK
 TOP_LEVELS = 7
 LOW_LEVELS = 3
 PLANES = 2**LOW_LEVELS - 1
+LEVEL9 = P * 4 - 1
 
 FLOPS = 2 * BATCH * FEATURES * 1024 + 2 * BATCH * LEAVES * CLASSES
 
@@ -32,7 +32,6 @@ def tile_treemodel_kernel(tc, x, W_gate, b_gate, leaf_logits, out):
     with ExitStack() as ctx:
         keep = ctx.enter_context(tc.tile_pool(name="keep", bufs=1))
         x_in = ctx.enter_context(tc.tile_pool(name="x_in", bufs=CHUNKS))
-        stage = ctx.enter_context(tc.tile_pool(name="stage", bufs=2))
         x_mx = ctx.enter_context(tc.tile_pool(name="x_mx", bufs=2))
         top = ctx.enter_context(tc.tile_pool(name="top", bufs=1))
         gates = ctx.enter_context(tc.tile_pool(name="gates", bufs=2))
@@ -47,6 +46,9 @@ def tile_treemodel_kernel(tc, x, W_gate, b_gate, leaf_logits, out):
 
         ident = keep.tile([P, P], F32)
         make_identity(nc, ident[:])
+        column = keep.tile([P, 1], F32)
+        nc.vector.memset(column[:], 0.0)
+        nc.scalar.activation(out=column[:], in_=column[:], func=SIGMOID)
         ones = keep.tile([P, P], BF16)
         nc.vector.memset(ones[:], 1.0)
         bias_top = keep.tile([P, P], BF16)
@@ -62,18 +64,28 @@ def tile_treemodel_kernel(tc, x, W_gate, b_gate, leaf_logits, out):
             )
 
         def load_x(c):
-            x_sb = x_in.tile([P, TILES, FEATURES], BF16)
+            x_sb = x_in.tile([P, TILES, FEATURES], BF16, name="x_sb")
             nc.sync.dma_start(out=x_sb[:].rearrange("p i k -> p (i k)"), in_=x_rows[c])
             return x_sb
 
-        x_chunks = [load_x(0)]
-        w_rows = []
-        for g in range(PASSES):
-            w_rows.append(keep.tile([P, PACK, 1023], BF16, name="w_rows%d" % g))
-            nc.sync.dma_start(
-                out=w_rows[g][:].rearrange("p (u e) n -> p u (e n)", e=2),
-                in_=W_gate.rearrange("(g u p e) n -> g p u (e n)", g=PASSES, p=P, e=2)[g],
-            )
+        def load_w(name, first_column):
+            w_sb = keep.tile([P, PASSES, 2, 2, BANK], BF16, name=name)
+            for g in range(PASSES):
+                for u in range(2):
+                    nc.sync.dma_start(
+                        out=w_sb[:, g, u],
+                        in_=W_gate.rearrange("(g u p e) n -> g u p e n", g=PASSES, u=2, e=2)[
+                            g, u, :, :, first_column : first_column + BANK
+                        ],
+                    )
+            return w_sb[:].rearrange("p g u e n -> p g (u e) n")
+
+        w_upper = load_w("w_upper", 0)
+        x_first = x_in.tile([P, TILES, FEATURES], BF16, name="x_sb")
+        for i in range(TILES):
+            nc.sync.dma_start(out=x_first[:, i, :], in_=x_rows[0][:, i * FEATURES : (i + 1) * FEATURES])
+        x_chunks = [x_first]
+        w_level9 = load_w("w_level9", LEVEL9)
         x_chunks.append(load_x(1))
         leaf_rows = keep.tile([P, 2 * PACK, CLASSES], BF16)
         nc.sync.dma_start(
@@ -111,50 +123,52 @@ def tile_treemodel_kernel(tc, x, W_gate, b_gate, leaf_logits, out):
         w_codes = keep.tile([P, PASSES, PLANES * P], U32, align_bytes=64)
         w_scales = keep.tile([P, PASSES, PLANES * P], U8, align_bytes=64)
 
-        def prepare_w():
-            grouped = []
-            for g in range(PASSES):
-                w_grouped = stage.tile([P, PLANES, P, PACK], BF16, align_bytes=64)
-                for a in range(LOW_LEVELS):
-                    planes = 2**a
-                    first_node = P * planes - 1
-                    copy = nc.vector.tensor_copy if a == LOW_LEVELS - 1 else nc.scalar.copy
-                    copy(
-                        out=w_grouped[:, planes - 1 : 2 * planes - 1],
-                        in_=w_rows[g][:, :, first_node : first_node + P * planes].rearrange(
-                            "p t (j m) -> p m j t", m=planes
-                        ),
-                    )
-                grouped.append(w_grouped)
-            for a in range(LOW_LEVELS):
-                for g in range(PASSES):
-                    planes = 2**a
-                    cols = slice((planes - 1) * P, (2 * planes - 1) * P)
-                    nc.vector.quantize_mx(
-                        out=w_codes[:, g, cols].bitcast(FP8X4),
-                        scales=w_scales[:, g, cols],
-                        in_=grouped[g][:, planes - 1 : 2 * planes - 1].rearrange("p m j t -> p (m j t)"),
-                    )
+        w_grouped = []
+        for g in range(PASSES):
+            w_grouped.append(keep.tile([P, PLANES, P, PACK], BF16, align_bytes=64, name="w_grouped%d" % g))
+
+        def regroup_w(copy, a, g):
+            planes = 2**a
+            first_column = 0 if a == LOW_LEVELS - 1 else P * planes - 1
+            w_sb = w_level9 if a == LOW_LEVELS - 1 else w_upper
+            for m in range(planes):
+                copy(
+                    out=w_grouped[g][:, planes - 1 + m].rearrange("p (n i) t -> p n t i", i=4),
+                    in_=w_sb[:, g, :, first_column : first_column + P * planes].rearrange(
+                        "p t (n i m) -> p m n t i", i=4, m=planes
+                    )[:, m],
+                )
+
+        def quantise_w(a, g):
+            planes = 2**a
+            cols = slice((planes - 1) * P, (2 * planes - 1) * P)
+            nc.vector.quantize_mx(
+                out=w_codes[:, g, cols].bitcast(FP8X4),
+                scales=w_scales[:, g, cols],
+                in_=w_grouped[g][:, planes - 1 : 2 * planes - 1].rearrange("p m j t -> p (m j t)"),
+            )
 
         leaf_codes = keep.tile([P, PASSES, CLASSES], U32, align_bytes=64)
         leaf_scales = keep.tile([P, PASSES, CLASSES], U8, align_bytes=64)
 
-        leaf_grouped = {}
+        leaf_grouped = []
+        for s in range(PASSES):
+            leaf_grouped.append(keep.tile([P, CLASSES, PACK], BF16, align_bytes=64, name="leaf_grouped%d" % s))
 
-        def regroup_leaves(s):
-            leaf_grouped[s] = stage.tile([P, CLASSES, PACK], BF16, align_bytes=64, name="leaf_grouped")
-            for h in range(CLASSES // BANK):
-                cols = slice(h * BANK, (h + 1) * BANK)
-                grouped = leaf_grouped[s][:, cols, :].rearrange("p (n i) t -> p n t i", i=4)
-                rows = (
-                    leaf_rows[:]
-                    .rearrange("p (t s) n -> p s t n", s=PASSES)[:, s, :, cols]
-                    .rearrange("p t (n i) -> p n t i", i=4)
-                )
-                if s == 0:
-                    nc.scalar.copy(out=grouped, in_=rows)
-                else:
-                    nc.scalar.mul(out=grouped, in_=rows, mul=-1.0)
+        def regroup_leaves(engine, s, quarter):
+            cols = slice(quarter * (CLASSES // 4), (quarter + 1) * (CLASSES // 4))
+            grouped = leaf_grouped[s][:, cols, :].rearrange("p (n i) t -> p n t i", i=4)
+            rows = (
+                leaf_rows[:]
+                .rearrange("p (t s) n -> p s t n", s=PASSES)[:, s, :, cols]
+                .rearrange("p t (n i) -> p n t i", i=4)
+            )
+            if engine is nc.vector:
+                nc.vector.tensor_copy(out=grouped, in_=rows)
+            elif s == 0:
+                nc.scalar.copy(out=grouped, in_=rows)
+            else:
+                nc.scalar.mul(out=grouped, in_=rows, mul=-1.0)
 
         def quantise_leaves(s):
             nc.vector.quantize_mx(
@@ -171,7 +185,7 @@ def tile_treemodel_kernel(tc, x, W_gate, b_gate, leaf_logits, out):
                         nc.tensor.matmul(
                             out=z_top[c][:, i, :],
                             lhsT=x_grouped[c][:, g, i * P : (i + 1) * P, t],
-                            rhs=w_rows[g][:, t, 0:P],
+                            rhs=w_upper[:, g, t, 0:P],
                             start=(g == 0 and t == 0),
                             stop=False,
                         )
@@ -200,9 +214,10 @@ def tile_treemodel_kernel(tc, x, W_gate, b_gate, leaf_logits, out):
             for i in range(TILES):
                 nc.tensor.transpose(reach7[c][:, i * P : (i + 1) * P], reach[c][:, i, :], ident[:])
 
-        def low_gates(c):
-            gate[c] = gates.tile([P, PLANES, CHUNK], F32, name="gate")
-            for a in range(LOW_LEVELS):
+        def low_gates(c, levels):
+            if 0 in levels:
+                gate[c] = gates.tile([P, PLANES, CHUNK], F32, name="gate")
+            for a in levels:
                 for m in range(2**a):
                     plane = 2**a - 1 + m
                     z = psum_ring.tile([P, CHUNK], F32, tag="ring")
@@ -250,8 +265,7 @@ def tile_treemodel_kernel(tc, x, W_gate, b_gate, leaf_logits, out):
             probs_codes[c] = probs_mx.tile([P, PASSES, CHUNK], U32, align_bytes=64, name="probs_codes")
             probs_scales[c] = probs_mx.tile([P, PASSES, CHUNK], U8, align_bytes=64, name="probs_scales")
 
-        def sweep_level_9(c, half, s):
-            rows = slice(half * HALF, (half + 1) * HALF)
+        def sweep_level_9(c, rows, s):
             right, parent = gate[c][:, 3:7, rows], minus_reach9[c][:, :, :, rows]
             words = probs_grouped[c][:, s, rows, :]
             if s == 0:
@@ -271,16 +285,15 @@ def tile_treemodel_kernel(tc, x, W_gate, b_gate, leaf_logits, out):
                     op=ALU.mult,
                 )
 
-        def quantise_probs(c, half, s):
-            rows = slice(half * HALF, (half + 1) * HALF)
+        def quantise_probs(c, rows, s):
             nc.vector.quantize_mx(
                 out=probs_codes[c][:, s, rows].bitcast(FP8X4),
                 scales=probs_scales[c][:, s, rows],
                 in_=probs_grouped[c][:, s, rows, :].rearrange("p b t -> p (b t)"),
             )
 
-        def leaf_product(c):
-            for i in range(TILES):
+        def leaf_product(c, tiles):
+            for i in tiles:
                 out_sb = result.tile([P, CLASSES], F32)
                 for h in range(CLASSES // BANK):
                     cols = slice(h * BANK, (h + 1) * BANK)
@@ -295,41 +308,75 @@ def tile_treemodel_kernel(tc, x, W_gate, b_gate, leaf_logits, out):
                             start=(s == 0),
                             stop=(s == PASSES - 1),
                         )
-                    nc.scalar.copy(out=out_sb[:, cols], in_=acc[:])
+                    if c == CHUNKS - 1 and i >= TILES // 2 and h == 1:
+                        nc.vector.tensor_copy(out=out_sb[:, cols], in_=acc[:])
+                    else:
+                        nc.scalar.copy(out=out_sb[:, cols], in_=acc[:])
                 nc.sync.dma_start(out=out_rows[c][:, i, :], in_=out_sb[:])
 
         def in_range(c):
             return 0 <= c < CHUNKS
 
+        def sweep_and_quantise(c, next_levels):
+            width = CHUNK // 2 if c < CHUNKS - 1 else P
+            pieces = []
+            for first in range(0, CHUNK, width):
+                rows = slice(first, first + width)
+                pieces += [(sweep_level_9, rows, s) for s in range(PASSES)]
+                pieces += [(quantise_probs, rows, s) for s in range(PASSES)]
+            next_levels = list(next_levels)
+            for n, (work, rows, s) in enumerate(pieces):
+                work(c, rows, s)
+                if n >= 1 and next_levels:
+                    top_level(c + 1, next_levels.pop(0))
+
         with tc.manual_schedule():
-            for c in range(-2, CHUNKS + 1):
+            for g in range(PASSES):
+                regroup_w(nc.vector.tensor_copy, 0, g)
+                regroup_w(nc.scalar.copy, 1, g)
+            for a in range(2):
+                for g in range(PASSES):
+                    quantise_w(a, g)
+            transpose_x(0)
+            quantise_x(0)
+            regroup_w(nc.scalar.copy, 2, 0)
+            regroup_w(nc.vector.tensor_copy, 2, 1)
+            top_logits(0)
+            top_turns(0)
+            for level in range(1, TOP_LEVELS):
+                top_level(0, level)
+                if level <= PASSES:
+                    quantise_w(2, level - 1)
+            low_gates(0, (0, 1))
+            top_transpose(0)
+            transpose_x(1)
+            low_gates(0, (2,))
+            for c in range(CHUNKS + 1):
                 if in_range(c):
                     sweep_levels_7_8(c)
                 if in_range(c + 1):
                     quantise_x(c + 1)
-                if c == -1:
-                    prepare_w()
                 if c == 1:
+                    for quarter in range(2):
+                        regroup_leaves(nc.vector, 0, quarter)
                     quantise_leaves(0)
                     quantise_leaves(1)
                 if in_range(c + 1):
                     top_logits(c + 1)
                     top_turns(c + 1)
-                    low_gates(c + 1)
-                for half in range(2):
-                    if in_range(c):
-                        for s in range(PASSES):
-                            sweep_level_9(c, half, s)
-                        for s in range(PASSES):
-                            quantise_probs(c, half, s)
-                    if in_range(c + 1) and half == 0:
-                        for level in range(1, TOP_LEVELS):
-                            top_level(c + 1, level)
-                if in_range(c - 1):
-                    leaf_product(c - 1)
-                if in_range(c + 1):
-                    top_transpose(c + 1)
+                    low_gates(c + 1, (0, 1))
                 if in_range(c + 2):
                     transpose_x(c + 2)
-                if c == -1 or c == 0:
-                    regroup_leaves(c + 1)
+                if c == 0:
+                    for s, quarter in ((0, 2), (0, 3), (1, 0), (1, 1), (1, 2), (1, 3)):
+                        regroup_leaves(nc.scalar, s, quarter)
+                if in_range(c - 1):
+                    leaf_product(c - 1, range(TILES // 2))
+                if in_range(c + 1):
+                    low_gates(c + 1, (2,))
+                if in_range(c):
+                    sweep_and_quantise(c, range(1, TOP_LEVELS) if in_range(c + 1) else ())
+                if in_range(c + 1):
+                    top_transpose(c + 1)
+                if in_range(c - 1):
+                    leaf_product(c - 1, range(TILES // 2, TILES))

@@ -18,6 +18,8 @@ BATCH, FEATURES, LEAVES, CLASSES = 2048, 1024, 1024, 1024
 PASSES = 2
 CHUNK = BANK
 TILES = CHUNK // P
+RUN = 4
+GROUPS = P // RUN
 CHUNKS = BATCH // CHUNK
 TOP_LEVELS = 7
 LOW_LEVELS = 3
@@ -46,6 +48,10 @@ def tile_treemodel_kernel(tc, x, W_gate, b_gate, leaf_logits, out):
 
         ident = keep.tile([P, P], F32)
         make_identity(nc, ident[:])
+        permute = keep.tile([P, P], F32)
+        nc.vector.tensor_copy(
+            out=permute[:].rearrange("p (g i) -> p g i", i=RUN), in_=ident[:].rearrange("p (i g) -> p g i", i=RUN)
+        )
         column = keep.tile([P, 1], F32)
         nc.vector.memset(column[:], 0.0)
         nc.scalar.activation(out=column[:], in_=column[:], func=SIGMOID)
@@ -94,7 +100,8 @@ def tile_treemodel_kernel(tc, x, W_gate, b_gate, leaf_logits, out):
         x_chunks.append(load_x(2))
         x_chunks.append(load_x(3))
 
-        x_grouped, x_codes, x_scales, z_top, turn, reach, reach7, gate = {}, {}, {}, {}, {}, {}, {}, {}
+        x_grouped, x_codes, x_scales, z_top, turn, reach, reach7 = {}, {}, {}, {}, {}, {}, {}
+        gate, gate9 = {}, {}
         minus_reach9, probs_grouped, probs_codes, probs_scales = {}, {}, {}, {}
 
         def transpose_x(c):
@@ -104,7 +111,7 @@ def tile_treemodel_kernel(tc, x, W_gate, b_gate, leaf_logits, out):
                 xt = psum_ring.tile([P, PASSES * 2, P], F32, tag="ring")
                 for j in range(PASSES * 2):
                     nc.tensor.transpose(
-                        xt[:, j, :], x_chunks[c][:, i, :].bitcast(F32)[:, j * P : (j + 1) * P], ident[:]
+                        xt[:, j, :], x_chunks[c][:, i, :].bitcast(F32)[:, j * P : (j + 1) * P], permute[:]
                     )
                 nc.scalar.copy(
                     out=x_pairs[:, :, i * P : (i + 1) * P, :], in_=xt[:].rearrange("p (g u) b -> p g b u", u=2)
@@ -165,10 +172,8 @@ def tile_treemodel_kernel(tc, x, W_gate, b_gate, leaf_logits, out):
             )
             if engine is nc.vector:
                 nc.vector.tensor_copy(out=grouped, in_=rows)
-            elif s == 0:
-                nc.scalar.copy(out=grouped, in_=rows)
             else:
-                nc.scalar.mul(out=grouped, in_=rows, mul=-1.0)
+                nc.scalar.copy(out=grouped, in_=rows)
 
         def quantise_leaves(s):
             nc.vector.quantize_mx(
@@ -216,7 +221,8 @@ def tile_treemodel_kernel(tc, x, W_gate, b_gate, leaf_logits, out):
 
         def low_gates(c, levels):
             if 0 in levels:
-                gate[c] = gates.tile([P, PLANES, CHUNK], F32, name="gate")
+                gate[c] = gates.tile([P, 3, CHUNK], F32, name="gate")
+                gate9[c] = gates.tile([P, TILES * GROUPS, PACK, RUN], F32, name="gate9")
             for a in levels:
                 for m in range(2**a):
                     plane = 2**a - 1 + m
@@ -232,7 +238,10 @@ def tile_treemodel_kernel(tc, x, W_gate, b_gate, leaf_logits, out):
                             stop=(g == PASSES - 1),
                         )
                     nc.scalar.activation(
-                        out=gate[c][:, plane, :], in_=z[:], func=SIGMOID, bias=bias_low[:, a, m : m + 1]
+                        out=gate9[c][:, :, m, :] if a == 2 else gate[c][:, plane, :].rearrange("p (g i) -> p g i", i=RUN),
+                        in_=z[:].rearrange("p (g i) -> p g i", i=RUN),
+                        func=SIGMOID,
+                        bias=bias_low[:, a, m : m + 1],
                     )
 
         def child_flipping_sign(s, child, p_right, parent):
@@ -249,41 +258,34 @@ def tile_treemodel_kernel(tc, x, W_gate, b_gate, leaf_logits, out):
             minus_reach8 = low.tile([P, 2, CHUNK], F32)
             for s3 in range(2):
                 child_flipping_sign(s3, minus_reach8[:, s3, :], gate[c][:, 0, :], reach7[c][:])
-            minus_reach9[c] = low.tile([P, 2, 2, CHUNK], F32, name="minus_reach9")
+            minus_reach9[c] = low.tile([P, TILES * GROUPS, 2, 2, RUN], F32, name="minus_reach9")
+            lines = minus_reach8[:].rearrange("p s3 (g i) -> p s3 g i", i=RUN)
             for s3 in range(2):
                 nc.vector.tensor_tensor(
-                    out=minus_reach9[c][:, s3, 1, :], in0=gate[c][:, 1 + s3, :], in1=minus_reach8[:, s3, :], op=ALU.mult
+                    out=minus_reach9[c][:, :, s3, 1, :],
+                    in0=gate[c][:, 1 + s3, :].rearrange("p (g i) -> p g i", i=RUN),
+                    in1=lines[:, s3],
+                    op=ALU.mult,
                 )
             for s3 in range(2):
                 nc.vector.tensor_tensor(
-                    out=minus_reach9[c][:, s3, 0, :],
-                    in0=minus_reach8[:, s3, :],
-                    in1=minus_reach9[c][:, s3, 1, :],
+                    out=minus_reach9[c][:, :, s3, 0, :],
+                    in0=lines[:, s3],
+                    in1=minus_reach9[c][:, :, s3, 1, :],
                     op=ALU.subtract,
                 )
             probs_grouped[c] = low.tile([P, PASSES, CHUNK, PACK], BF16, align_bytes=64, name="probs_grouped")
             probs_codes[c] = probs_mx.tile([P, PASSES, CHUNK], U32, align_bytes=64, name="probs_codes")
             probs_scales[c] = probs_mx.tile([P, PASSES, CHUNK], U8, align_bytes=64, name="probs_scales")
 
-        def sweep_level_9(c, rows, s):
-            right, parent = gate[c][:, 3:7, rows], minus_reach9[c][:, :, :, rows]
-            words = probs_grouped[c][:, s, rows, :]
-            if s == 0:
-                nc.vector.scalar_tensor_tensor(
-                    out=words,
-                    in0=right.rearrange("p t b -> p b t"),
-                    scalar=1.0,
-                    in1=parent.rearrange("p s3 s2 b -> p b (s3 s2)"),
-                    op0=ALU.subtract,
-                    op1=ALU.mult,
-                )
-            else:
-                nc.vector.tensor_tensor(
-                    out=words.rearrange("p (b i) t -> p b t i", i=4),
-                    in0=right.rearrange("p t (b i) -> p b t i", i=4),
-                    in1=parent.rearrange("p s3 s2 (b i) -> p b (s3 s2) i", i=4),
-                    op=ALU.mult,
-                )
+        def sweep_level_9(c, tile, s):
+            groups = slice(tile * GROUPS, (tile + 1) * GROUPS)
+            child_flipping_sign(
+                s,
+                probs_grouped[c][:, s, tile * P : (tile + 1) * P, :].rearrange("p (i g) t -> p (g t) i", i=RUN),
+                gate9[c][:, groups].rearrange("p g t i -> p (g t) i"),
+                minus_reach9[c][:, groups].rearrange("p g s3 s2 i -> p (g s3 s2) i"),
+            )
 
         def quantise_probs(c, rows, s):
             nc.vector.quantize_mx(
@@ -318,16 +320,16 @@ def tile_treemodel_kernel(tc, x, W_gate, b_gate, leaf_logits, out):
             return 0 <= c < CHUNKS
 
         def sweep_and_quantise(c, next_levels):
-            width = CHUNK // 2 if c < CHUNKS - 1 else P
+            width = 2 if c < CHUNKS - 1 else 1
             pieces = []
-            for first in range(0, CHUNK, width):
-                rows = slice(first, first + width)
-                pieces += [(sweep_level_9, rows, s) for s in range(PASSES)]
+            for first in range(0, TILES, width):
+                rows = slice(first * P, (first + width) * P)
+                pieces += [(sweep_level_9, first + n, s) for n in range(width) for s in range(PASSES)]
                 pieces += [(quantise_probs, rows, s) for s in range(PASSES)]
             next_levels = list(next_levels)
-            for n, (work, rows, s) in enumerate(pieces):
-                work(c, rows, s)
-                if n >= 1 and next_levels:
+            for n, (work, where, s) in enumerate(pieces):
+                work(c, where, s)
+                if n >= 3 and next_levels:
                     top_level(c + 1, next_levels.pop(0))
 
         with tc.manual_schedule():

@@ -86,11 +86,11 @@ def tile_treemodel_kernel(tc, x, W_gate, b_gate, leaf_logits, out):
                     )
             return w_sb[:].rearrange("p g u e n -> p g (u e) n")
 
-        w_upper = load_w("w_upper", 0)
         x_first = x_in.tile([P, TILES, FEATURES], BF16, name="x_sb")
         for i in range(TILES):
             nc.sync.dma_start(out=x_first[:, i, :], in_=x_rows[0][:, i * FEATURES : (i + 1) * FEATURES])
         x_chunks = [x_first]
+        w_upper = load_w("w_upper", 0)
         w_level9 = load_w("w_level9", LEVEL9)
         x_chunks.append(load_x(1))
         leaf_rows = keep.tile([P, 2 * PACK, CLASSES], BF16)
@@ -333,18 +333,18 @@ def tile_treemodel_kernel(tc, x, W_gate, b_gate, leaf_logits, out):
                     top_level(c + 1, next_levels.pop(0))
 
         with tc.manual_schedule():
+            transpose_x(0)
+            quantise_x(0)
             for g in range(PASSES):
                 regroup_w(nc.vector.tensor_copy, 0, g)
                 regroup_w(nc.scalar.copy, 1, g)
             for a in range(2):
                 for g in range(PASSES):
                     quantise_w(a, g)
-            transpose_x(0)
-            quantise_x(0)
-            regroup_w(nc.scalar.copy, 2, 0)
-            regroup_w(nc.vector.tensor_copy, 2, 1)
             top_logits(0)
             top_turns(0)
+            regroup_w(nc.scalar.copy, 2, 0)
+            regroup_w(nc.vector.tensor_copy, 2, 1)
             for level in range(1, TOP_LEVELS):
                 top_level(0, level)
                 if level <= PASSES:
@@ -366,19 +366,24 @@ def tile_treemodel_kernel(tc, x, W_gate, b_gate, leaf_logits, out):
                 if in_range(c + 1):
                     top_logits(c + 1)
                     top_turns(c + 1)
+                    if c == 0:
+                        regroup_leaves(nc.scalar, 0, 2)
+                        regroup_leaves(nc.scalar, 0, 3)
                     low_gates(c + 1, (0, 1))
+                    if c == 0:
+                        regroup_leaves(nc.scalar, 1, 0)
+                        regroup_leaves(nc.scalar, 1, 1)
+                if in_range(c - 1):
+                    leaf_product(c - 1, range(TILES // 2))
                 if in_range(c + 2):
                     transpose_x(c + 2)
                 if c == 0:
-                    for s, quarter in ((0, 2), (0, 3), (1, 0), (1, 1), (1, 2), (1, 3)):
-                        regroup_leaves(nc.scalar, s, quarter)
+                    regroup_leaves(nc.scalar, 1, 2)
+                    regroup_leaves(nc.scalar, 1, 3)
                 if in_range(c - 1):
-                    leaf_product(c - 1, range(TILES // 2))
-                if in_range(c + 1):
-                    low_gates(c + 1, (2,))
+                    leaf_product(c - 1, range(TILES // 2, TILES))
                 if in_range(c):
                     sweep_and_quantise(c, range(1, TOP_LEVELS) if in_range(c + 1) else ())
                 if in_range(c + 1):
                     top_transpose(c + 1)
-                if in_range(c - 1):
-                    leaf_product(c - 1, range(TILES // 2, TILES))
+                    low_gates(c + 1, (2,))

@@ -113,7 +113,8 @@ def tile_treemodel_kernel(tc, x, W_gate, b_gate, leaf_logits, out):
                     nc.tensor.transpose(
                         xt[:, j, :], x_chunks[c][:, i, :].bitcast(F32)[:, j * P : (j + 1) * P], permute[:]
                     )
-                nc.scalar.copy(
+                copy = nc.vector.tensor_copy if c == 0 and i % 2 == 1 else nc.scalar.copy
+                copy(
                     out=x_pairs[:, :, i * P : (i + 1) * P, :], in_=xt[:].rearrange("p (g u) b -> p g b u", u=2)
                 )
 
@@ -347,8 +348,9 @@ def tile_treemodel_kernel(tc, x, W_gate, b_gate, leaf_logits, out):
             regroup_w(nc.vector.tensor_copy, 2, 1)
             for level in range(1, TOP_LEVELS):
                 top_level(0, level)
-                if level <= PASSES:
-                    quantise_w(2, level - 1)
+                if level == 1:
+                    quantise_w(2, 1)
+            quantise_w(2, 0)
             low_gates(0, (0, 1))
             top_transpose(0)
             transpose_x(1)

from contextlib import ExitStack

import concourse.mybir as mybir
from concourse.masks import make_identity

F32 = mybir.dt.float32
BF16 = mybir.dt.bfloat16
U32 = mybir.dt.uint32
U8 = mybir.dt.uint8
FP8X4 = mybir.dt.float8_e4m3fn_x4
ALU = mybir.AluOpType
SIGMOID = mybir.ActivationFunctionType.Sigmoid

P = 128
PACK = 4
BANK = 512
BATCH, FEATURES, LEAVES, CLASSES = 2048, 1024, 1024, 1024
PASSES = 2
CHUNK = BANK
TILES = CHUNK // P
RUN = 4
GROUPS = P // RUN
CHUNKS = BATCH // CHUNK
TOP_LEVELS = 7
LOW_LEVELS = 3
PLANES = 2**LOW_LEVELS - 1
LEVEL9 = P * 4 - 1

FLOPS = 2 * BATCH * FEATURES * 1024 + 2 * BATCH * LEAVES * CLASSES


def tile_treemodel_kernel(tc, x, W_gate, b_gate, leaf_logits, out):
    nc = tc.nc
    with ExitStack() as ctx:
        keep = ctx.enter_context(tc.tile_pool(name="keep", bufs=1))
        x_in = ctx.enter_context(tc.tile_pool(name="x_in", bufs=CHUNKS))
        x_mx = ctx.enter_context(tc.tile_pool(name="x_mx", bufs=2))
        top = ctx.enter_context(tc.tile_pool(name="top", bufs=1))
        gates = ctx.enter_context(tc.tile_pool(name="gates", bufs=2))
        low = ctx.enter_context(tc.tile_pool(name="low", bufs=1))
        probs_mx = ctx.enter_context(tc.tile_pool(name="probs_mx", bufs=2))
        result = ctx.enter_context(tc.tile_pool(name="result", bufs=4))
        psum_top = ctx.enter_context(tc.psum_pool(name="psum_top", bufs=1))
        psum_ring = ctx.enter_context(tc.psum_pool(name="psum_ring", bufs=6))

        x_rows = x.rearrange("(c p i) k -> c p (i k)", p=P, i=TILES)
        out_rows = out.rearrange("(c p i) n -> c p i n", p=P, i=TILES)

        ident = keep.tile([P, P], F32)
        make_identity(nc, ident[:])
        permute = keep.tile([P, P], F32)
        nc.vector.tensor_copy(
            out=permute[:].rearrange("p (g i) -> p g i", i=RUN), in_=ident[:].rearrange("p (i g) -> p g i", i=RUN)
        )
        column = keep.tile([P, 1], F32)
        nc.vector.memset(column[:], 0.0)
        nc.scalar.activation(out=column[:], in_=column[:], func=SIGMOID)
        ones = keep.tile([P, P], BF16)
        nc.vector.memset(ones[:], 1.0)
        bias_top = keep.tile([P, P], BF16)
        nc.vector.memset(bias_top[:], 0.0)
        nc.scalar.dma_start(out=bias_top[0:1, :], in_=b_gate[0:P].rearrange("(o n) -> o n", o=1))
        bias_low = keep.tile([P, LOW_LEVELS, 16], BF16)
        for a in range(LOW_LEVELS):
            planes = 2**a
            first_node = P * planes - 1
            nc.scalar.dma_start(
                out=bias_low[:, a, 0:planes],
                in_=b_gate[first_node : first_node + P * planes].rearrange("(p m) -> p m", m=planes),
            )

        def load_x(c):
            x_sb = x_in.tile([P, TILES, FEATURES], BF16, name="x_sb")
            nc.sync.dma_start(out=x_sb[:].rearrange("p i k -> p (i k)"), in_=x_rows[c])
            return x_sb

        def load_w(name, first_column):
            w_sb = keep.tile([P, PASSES, 2, 2, BANK], BF16, name=name)
            for g in range(PASSES):
                for u in range(2):
                    nc.sync.dma_start(
                        out=w_sb[:, g, u],
                        in_=W_gate.rearrange("(g u p e) n -> g u p e n", g=PASSES, u=2, e=2)[
                            g, u, :, :, first_column : first_column + BANK
                        ],
                    )
            return w_sb[:].rearrange("p g u e n -> p g (u e) n")

        x_first = x_in.tile([P, TILES, FEATURES], BF16, name="x_sb")
        for i in range(TILES):
            nc.sync.dma_start(out=x_first[:, i, :], in_=x_rows[0][:, i * FEATURES : (i + 1) * FEATURES])
        x_chunks = [x_first]
        w_upper = load_w("w_upper", 0)
        w_level9 = load_w("w_level9", LEVEL9)
        x_chunks.append(load_x(1))
        leaf_rows = keep.tile([P, 2 * PACK, CLASSES], BF16)
        nc.sync.dma_start(
            out=leaf_rows[:].rearrange("p r n -> p (r n)"), in_=leaf_logits.rearrange("(p r) n -> p (r n)", p=P)
        )
        x_chunks.append(load_x(2))
        x_chunks.append(load_x(3))

        x_grouped, x_codes, x_scales, z_top, turn, reach, reach7 = {}, {}, {}, {}, {}, {}, {}
        gate, gate9 = {}, {}
        minus_reach9, probs_grouped, probs_codes, probs_scales = {}, {}, {}, {}

        def transpose_x(c):
            x_grouped[c] = x_mx.tile([P, PASSES, CHUNK, PACK], BF16, align_bytes=64, name="x_grouped")
            x_pairs = x_grouped[c][:].bitcast(F32)
            for i in range(TILES):
                xt = psum_ring.tile([P, PASSES * 2, P], F32, tag="ring")
                for j in range(PASSES * 2):
                    nc.tensor.transpose(
                        xt[:, j, :], x_chunks[c][:, i, :].bitcast(F32)[:, j * P : (j + 1) * P], permute[:]
                    )
                copy = nc.vector.tensor_copy if c == 0 and i % 2 == 1 else nc.scalar.copy
                copy(
                    out=x_pairs[:, :, i * P : (i + 1) * P, :], in_=xt[:].rearrange("p (g u) b -> p g b u", u=2)
                )

        def quantise_x(c):
            x_codes[c] = x_mx.tile([P, PASSES, CHUNK], U32, align_bytes=64, name="x_codes")
            x_scales[c] = x_mx.tile([P, PASSES, CHUNK], U8, align_bytes=64, name="x_scales")
            for g in range(PASSES):
                nc.vector.quantize_mx(
                    out=x_codes[c][:, g, :].bitcast(FP8X4),
                    scales=x_scales[c][:, g, :],
                    in_=x_grouped[c][:, g].rearrange("p b t -> p (b t)"),
                )

        w_codes = keep.tile([P, PASSES, PLANES * P], U32, align_bytes=64)
        w_scales = keep.tile([P, PASSES, PLANES * P], U8, align_bytes=64)

        w_grouped = []
        for g in range(PASSES):
            w_grouped.append(keep.tile([P, PLANES, P, PACK], BF16, align_bytes=64, name="w_grouped%d" % g))

        def regroup_w(copy, a, g):
            planes = 2**a
            first_column = 0 if a == LOW_LEVELS - 1 else P * planes - 1
            w_sb = w_level9 if a == LOW_LEVELS - 1 else w_upper
            for m in range(planes):
                copy(
                    out=w_grouped[g][:, planes - 1 + m].rearrange("p (n i) t -> p n t i", i=4),
                    in_=w_sb[:, g, :, first_column : first_column + P * planes].rearrange(
                        "p t (n i m) -> p m n t i", i=4, m=planes
                    )[:, m],
                )

        def quantise_w(a, g):
            planes = 2**a
            cols = slice((planes - 1) * P, (2 * planes - 1) * P)
            nc.vector.quantize_mx(
                out=w_codes[:, g, cols].bitcast(FP8X4),
                scales=w_scales[:, g, cols],
                in_=w_grouped[g][:, planes - 1 : 2 * planes - 1].rearrange("p m j t -> p (m j t)"),
            )

        leaf_codes = keep.tile([P, PASSES, CLASSES], U32, align_bytes=64)
        leaf_scales = keep.tile([P, PASSES, CLASSES], U8, align_bytes=64)

        leaf_grouped = []
        for s in range(PASSES):
            leaf_grouped.append(keep.tile([P, CLASSES, PACK], BF16, align_bytes=64, name="leaf_grouped%d" % s))

        def regroup_leaves(engine, s, quarter):
            cols = slice(quarter * (CLASSES // 4), (quarter + 1) * (CLASSES // 4))
            grouped = leaf_grouped[s][:, cols, :].rearrange("p (n i) t -> p n t i", i=4)
            rows = (
                leaf_rows[:]
                .rearrange("p (t s) n -> p s t n", s=PASSES)[:, s, :, cols]
                .rearrange("p t (n i) -> p n t i", i=4)
            )
            if engine is nc.vector:
                nc.vector.tensor_copy(out=grouped, in_=rows)
            else:
                nc.scalar.copy(out=grouped, in_=rows)

        def quantise_leaves(s):
            nc.vector.quantize_mx(
                out=leaf_codes[:, s, :].bitcast(FP8X4),
                scales=leaf_scales[:, s, :],
                in_=leaf_grouped[s][:].rearrange("p n t -> p (n t)"),
            )

        def top_logits(c):
            z_top[c] = psum_top.tile([P, TILES, P], F32, name="z_top")
            for i in range(TILES):
                for g in range(PASSES):
                    for t in range(PACK):
                        nc.tensor.matmul(
                            out=z_top[c][:, i, :],
                            lhsT=x_grouped[c][:, g, i * P : (i + 1) * P, t],
                            rhs=w_upper[:, g, t, 0:P],
                            start=(g == 0 and t == 0),
                            stop=False,
                        )
                nc.tensor.matmul(out=z_top[c][:, i, :], lhsT=ones[:], rhs=bias_top[:], start=False, stop=True)

        def top_turns(c):
            turn[c] = top.tile([P, 2, TILES, P], F32, name="turn")
            nc.scalar.activation(out=turn[c][:, 1], in_=z_top[c][:], func=SIGMOID)
            nc.scalar.activation(out=turn[c][:, 0], in_=z_top[c][:], func=SIGMOID, scale=-1.0)

        def top_level(c, level):
            n = 2**level
            if level == 1:
                reach[c] = turn[c][:, :, :, 0].rearrange("p s i -> p i s")
            children = top.tile([P, TILES, n, 2], F32, name="children%d" % level)
            nc.vector.tensor_tensor(
                out=children[:],
                in0=turn[c][:, :, :, n - 1 : 2 * n - 1].rearrange("p s i j -> p i j s"),
                in1=reach[c].unsqueeze(3).to_broadcast([P, TILES, n, 2]),
                op=ALU.mult,
            )
            reach[c] = children[:].rearrange("p i j s -> p i (j s)")

        def top_transpose(c):
            reach7[c] = psum_top.tile([P, CHUNK], F32, name="reach7")
            for i in range(TILES):
                nc.tensor.transpose(reach7[c][:, i * P : (i + 1) * P], reach[c][:, i, :], ident[:])

        def low_gates(c, levels):
            if 0 in levels:
                gate[c] = gates.tile([P, 3, CHUNK], F32, name="gate")
                gate9[c] = gates.tile([P, TILES * GROUPS, PACK, RUN], F32, name="gate9")
            for a in levels:
                for m in range(2**a):
                    plane = 2**a - 1 + m
                    z = psum_ring.tile([P, CHUNK], F32, tag="ring")
                    for g in range(PASSES):
                        nc.tensor.matmul_mx(
                            out=z[:],
                            lhsT=w_codes[:, g, plane * P : (plane + 1) * P].bitcast(FP8X4),
                            lhsT_scale=w_scales[:, g, plane * P : (plane + 1) * P],
                            rhs=x_codes[c][:, g, :].bitcast(FP8X4),
                            rhs_scale=x_scales[c][:, g, :],
                            start=(g == 0),
                            stop=(g == PASSES - 1),
                        )
                    nc.scalar.activation(
                        out=gate9[c][:, :, m, :] if a == 2 else gate[c][:, plane, :].rearrange("p (g i) -> p g i", i=RUN),
                        in_=z[:].rearrange("p (g i) -> p g i", i=RUN),
                        func=SIGMOID,
                        bias=bias_low[:, a, m : m + 1],
                    )

        def child_flipping_sign(s, child, p_right, parent):
            if s == 0:
                nc.vector.scalar_tensor_tensor(
                    out=child, in0=p_right, scalar=1.0, in1=parent, op0=ALU.subtract, op1=ALU.mult
                )
            else:
                nc.vector.scalar_tensor_tensor(
                    out=child, in0=p_right, scalar=-1.0, in1=parent, op0=ALU.mult, op1=ALU.mult
                )

        def sweep_levels_7_8(c):
            minus_reach8 = low.tile([P, 2, CHUNK], F32)
            for s3 in range(2):
                child_flipping_sign(s3, minus_reach8[:, s3, :], gate[c][:, 0, :], reach7[c][:])
            minus_reach9[c] = low.tile([P, TILES * GROUPS, 2, 2, RUN], F32, name="minus_reach9")
            lines = minus_reach8[:].rearrange("p s3 (g i) -> p s3 g i", i=RUN)
            for s3 in range(2):
                nc.vector.tensor_tensor(
                    out=minus_reach9[c][:, :, s3, 1, :],
                    in0=gate[c][:, 1 + s3, :].rearrange("p (g i) -> p g i", i=RUN),
                    in1=lines[:, s3],
                    op=ALU.mult,
                )
            for s3 in range(2):
                nc.vector.tensor_tensor(
                    out=minus_reach9[c][:, :, s3, 0, :],
                    in0=lines[:, s3],
                    in1=minus_reach9[c][:, :, s3, 1, :],
                    op=ALU.subtract,
                )
            probs_grouped[c] = low.tile([P, PASSES, CHUNK, PACK], BF16, align_bytes=64, name="probs_grouped")
            probs_codes[c] = probs_mx.tile([P, PASSES, CHUNK], U32, align_bytes=64, name="probs_codes")
            probs_scales[c] = probs_mx.tile([P, PASSES, CHUNK], U8, align_bytes=64, name="probs_scales")

        def sweep_level_9(c, tile, s):
            groups = slice(tile * GROUPS, (tile + 1) * GROUPS)
            child_flipping_sign(
                s,
                probs_grouped[c][:, s, tile * P : (tile + 1) * P, :].rearrange("p (i g) t -> p (g t) i", i=RUN),
                gate9[c][:, groups].rearrange("p g t i -> p (g t) i"),
                minus_reach9[c][:, groups].rearrange("p g s3 s2 i -> p (g s3 s2) i"),
            )

        def quantise_probs(c, rows, s):
            nc.vector.quantize_mx(
                out=probs_codes[c][:, s, rows].bitcast(FP8X4),
                scales=probs_scales[c][:, s, rows],
                in_=probs_grouped[c][:, s, rows, :].rearrange("p b t -> p (b t)"),
            )

        def leaf_product(c, tiles):
            for i in tiles:
                out_sb = result.tile([P, CLASSES], F32)
                for h in range(CLASSES // BANK):
                    cols = slice(h * BANK, (h + 1) * BANK)
                    acc = psum_ring.tile([P, BANK], F32, tag="ring")
                    for s in range(PASSES):
                        nc.tensor.matmul_mx(
                            out=acc[:],
                            lhsT=probs_codes[c][:, s, i * P : (i + 1) * P].bitcast(FP8X4),
                            lhsT_scale=probs_scales[c][:, s, i * P : (i + 1) * P],
                            rhs=leaf_codes[:, s, cols].bitcast(FP8X4),
                            rhs_scale=leaf_scales[:, s, cols],
                            start=(s == 0),
                            stop=(s == PASSES - 1),
                        )
                    if c == CHUNKS - 1 and i >= TILES // 2 and h == 1:
                        nc.vector.tensor_copy(out=out_sb[:, cols], in_=acc[:])
                    else:
                        nc.scalar.copy(out=out_sb[:, cols], in_=acc[:])
                nc.sync.dma_start(out=out_rows[c][:, i, :], in_=out_sb[:])

        def in_range(c):
            return 0 <= c < CHUNKS

        def sweep_and_quantise(c, next_levels):
            width = 2 if c < CHUNKS - 1 else 1
            pieces = []
            for first in range(0, TILES, width):
                rows = slice(first * P, (first + width) * P)
                pieces += [(sweep_level_9, first + n, s) for n in range(width) for s in range(PASSES)]
                pieces += [(quantise_probs, rows, s) for s in range(PASSES)]
            next_levels = list(next_levels)
            for n, (work, where, s) in enumerate(pieces):
                work(c, where, s)
                if n >= 3 and next_levels:
                    top_level(c + 1, next_levels.pop(0))

        with tc.manual_schedule():
            transpose_x(0)
            quantise_x(0)
            for g in range(PASSES):
                regroup_w(nc.vector.tensor_copy, 0, g)
                regroup_w(nc.scalar.copy, 1, g)
            for a in range(2):
                for g in range(PASSES):
                    quantise_w(a, g)
            top_logits(0)
            top_turns(0)
            regroup_w(nc.scalar.copy, 2, 0)
            regroup_w(nc.vector.tensor_copy, 2, 1)
            for level in range(1, TOP_LEVELS):
                top_level(0, level)
                if level == 1:
                    quantise_w(2, 1)
            quantise_w(2, 0)
            low_gates(0, (0, 1))
            top_transpose(0)
            transpose_x(1)
            low_gates(0, (2,))
            for c in range(CHUNKS + 1):
                if in_range(c):
                    sweep_levels_7_8(c)
                if in_range(c + 1):
                    quantise_x(c + 1)
                if c == 1:
                    for quarter in range(2):
                        regroup_leaves(nc.vector, 0, quarter)
                    quantise_leaves(0)
                    quantise_leaves(1)
                if in_range(c + 1):
                    top_logits(c + 1)
                    top_turns(c + 1)
                    if c == 0:
                        regroup_leaves(nc.scalar, 0, 2)
                        regroup_leaves(nc.scalar, 0, 3)
                    low_gates(c + 1, (0, 1))
                    if c == 0:
                        regroup_leaves(nc.scalar, 1, 0)
                        regroup_leaves(nc.scalar, 1, 1)
                if in_range(c - 1):
                    leaf_product(c - 1, range(TILES // 2))
                if in_range(c + 2):
                    transpose_x(c + 2)
                if c == 0:
                    regroup_leaves(nc.scalar, 1, 2)
                    regroup_leaves(nc.scalar, 1, 3)
                if in_range(c - 1):
                    leaf_product(c - 1, range(TILES // 2, TILES))
                if in_range(c):
                    sweep_and_quantise(c, range(1, TOP_LEVELS) if in_range(c + 1) else ())
                if in_range(c + 1):
                    top_transpose(c + 1)
                    low_gates(c + 1, (2,))
